import numpy as np
import ml_dtypes


BF16 = ml_dtypes.bfloat16


def bf(x):
    return np.asarray(x, np.float32).astype(BF16)


def f64(x):
    return np.asarray(x).astype(np.float64)


E2M1 = np.array([0.0, 0.5, 1.0, 1.5, 2.0, 3.0, 4.0, 6.0, -0.0, -0.5, -1.0, -1.5, -2.0, -3.0, -4.0, -6.0])


def pack_weight(w, fmt):
    k, n = w.shape
    w = f64(bf(w)).reshape(k // 32, 32, n)
    amax = np.abs(w).max(1)
    if fmt == "e4m3":
        byte = np.frexp(amax)[1] - 1 + 127 - 7
    else:
        mant, ex = np.frexp(amax / 6.0)
        byte = np.where(mant > 0.5, ex, ex - 1) + 127
    byte = np.clip(np.where(amax > 0, byte, 1), 1, 254)
    scaled = (w * np.exp2(127.0 - byte)[:, None, :]).reshape(k, n).astype(np.float32)
    by_word = np.ascontiguousarray(scaled.reshape(k // 512, 128, 4, n).transpose(0, 1, 3, 2))
    if fmt == "e4m3":
        words = by_word.astype(ml_dtypes.float8_e4m3fn).view(np.uint8)
    else:
        c = by_word.astype(ml_dtypes.float4_e2m1fn).view(np.uint8) & 0xF
        words = c[..., 0::2] | (c[..., 1::2] << 4)
    return np.ascontiguousarray(words), np.ascontiguousarray(byte.astype(np.uint8).reshape(k // 512, 16, n))


def unpack_weight(words, scales, fmt):
    g, p, n, _ = words.shape
    if fmt == "e4m3":
        vals = np.ascontiguousarray(words).view(ml_dtypes.float8_e4m3fn).astype(np.float64)
    else:
        nib = np.empty((g, p, n, 4), np.uint8)
        nib[..., 0::2] = words & 0xF
        nib[..., 1::2] = words >> 4
        vals = E2M1[nib]
    vals = vals * np.repeat(np.exp2(scales.astype(np.float64) - 127.0), 8, axis=1)[..., None]
    return vals.transpose(0, 1, 3, 2).reshape(g * 512, n)

def pack4(w):
    words, scales = pack_weight(w, "e2m1")
    return words.reshape(words.shape[0], 128, -1), scales


def unpack4(words, scales):
    return unpack_weight(words.reshape(words.shape[0], 128, -1, 2), scales, "e2m1")


def kspread(k):
    return np.exp2(np.repeat(np.random.randint(-6, 7, k // 32), 32).astype(np.float64))


B, I, H = 256, 1536, 1024


def sig(v):
    return 1.0 / (1.0 + np.exp(-v))


def setup_inputs():
    s, t = kspread(I), kspread(H)
    x = np.random.standard_normal((B, I)) * s
    x_words, x_scales = pack4(x.T)
    m_prev = np.random.standard_normal((B, H)) * t
    m_prev_words, m_prev_scales = pack4(m_prev.T)
    c_prev = bf(np.random.standard_normal((B, H)))
    w_m_words, w_m_scales = pack4(np.random.standard_normal((H, 8 * H)) / np.sqrt(H) / t[:, None])
    w_inputs_words, w_inputs_scales = pack4(np.random.standard_normal((I, 8 * H)) / np.sqrt(I) / s[:, None])
    return {"x_words": x_words,
            "x_scales": x_scales,
            "m_prev_words": m_prev_words,
            "m_prev_scales": m_prev_scales,
            "c_prev": c_prev,
            "w_m_words": w_m_words,
            "w_m_scales": w_m_scales,
            "w_inputs_words": w_inputs_words,
            "w_inputs_scales": w_inputs_scales}


def reference(x_words, x_scales, m_prev_words, m_prev_scales, c_prev, w_m_words, w_m_scales, w_inputs_words, w_inputs_scales):
    m_mat = unpack4(m_prev_words, m_prev_scales).T @ unpack4(w_m_words, w_m_scales)
    in_mat = unpack4(x_words, x_scales).T @ unpack4(w_inputs_words, w_inputs_scales)
    ms = np.split(m_mat, 8, axis=1)
    xs = np.split(in_mat, 8, axis=1)
    l1_0 = sig(xs[0] + ms[0])
    l1_1 = np.maximum(xs[1] + ms[1], 0.0)
    l1_2 = sig(xs[2] + ms[2])
    l1_3 = np.maximum(xs[3] * ms[3], 0.0)
    l1_4 = np.tanh(xs[4] + ms[4])
    l1_5 = sig(xs[5] + ms[5])
    l1_6 = np.tanh(xs[6] + ms[6])
    l1_7 = sig(xs[7] + ms[7])
    l2_0 = np.tanh(l1_0 * l1_1)
    l2_1 = np.tanh(l1_2 + l1_3)
    l2_2 = np.tanh(l1_4 * l1_5)
    l2_3 = sig(l1_6 + l1_7)
    l2_0 = np.tanh(l2_0 + f64(c_prev))
    new_c = l2_0 * l2_1
    l3_1 = np.tanh(l2_2 + l2_3)
    new_m = np.tanh(new_c * l3_1)
    return (new_m, new_c)

@@ -1,0 +1,270 @@
+from contextlib import ExitStack
+
+import concourse.mybir as mybir
+
+F32 = mybir.dt.float32
+BF16 = mybir.dt.bfloat16
+I32 = mybir.dt.int32
+U8 = mybir.dt.uint8
+F4X4 = mybir.dt.float4_e2m1fn_x4
+ACT = mybir.ActivationFunctionType
+ALU = mybir.AluOpType
+
+B, I, H = 256, 1536, 1024
+FLOPS = 2 * B * 8 * H * (I + H)
+
+P = 128
+GM, GX = H // 512, I // 512
+HALF = 512
+WARM = 12
+
+
+def tile_nascell_kernel(tc, x_words, x_scales, m_words, m_scales, c_prev,
+                                    wm_words, wm_scales, wx_words, wx_scales, new_m, new_c):
+    nc = tc.nc
+    with ExitStack() as ctx:
+        keep = ctx.enter_context(tc.tile_pool(name="keep", bufs=1))
+        work = ctx.enter_context(tc.tile_pool(name="work", bufs=2))
+        psum = ctx.enter_context(tc.psum_pool(name="psum", bufs=8))
+        ctx.enter_context(tc.manual_schedule())
+
+        words, planes = {}, {}
+        tensors = {"m": (m_words, m_scales, wm_words, wm_scales, GM),
+                   "x": (x_words, x_scales, wx_words, wx_scales, GX)}
+        sets = ((2, 2), (0, 2), (4, 4))
+        set_of = {}
+        for s in range(len(sets)):
+            for j in range(sets[s][0], sets[s][0] + sets[s][1]):
+                set_of[j] = s
+        for op in ("m", "x"):
+            g_n = tensors[op][4]
+            t_w = keep.tile([P, g_n, 2 * B], U8, name="aw_" + op, align_bytes=64)
+            words[op] = t_w
+            t_p = keep.tile([P, g_n, B], U8, name="ap_" + op, align_bytes=64)
+            planes[op] = t_p
+            for s in range(len(sets)):
+                t_s = keep.tile([P, g_n, sets[s][1] * H], U8, name="wp_%s%d" % (op, s), align_bytes=64)
+                planes[(op, s)] = t_s
+            for j in range(8):
+                for h in range(2):
+                    t_ww = keep.tile([P, g_n, 2 * HALF], U8, name="ww_%s%d%d" % (op, j, h), align_bytes=64)
+                    words[(op, j, h)] = t_ww
+        m3 = keep.tile([P, 2, H], F32, name="m3")
+        cp = keep.tile([P, 2, H], BF16, name="cp")
+        zero = keep.tile([P, 512], BF16, name="zero")
+        warm = keep.tile([P, 8], F32, name="warm")
+
+        def zero_planes(engine, tile, g0, g1):
+            engine.memset(tile[:, g0:g1, :].rearrange("p g n -> p (g n)").bitcast(I32), 0)
+
+        def load_scales(dst, src, c0, c1):
+            for q in range(4):
+                nc.sync.dma_start(
+                    out=dst[32 * q : 32 * q + 4, :, :].bitcast(I32),
+                    in_=src[:, 4 * q : 4 * q + 4, c0:c1].rearrange("g r n -> r g n").bitcast(I32))
+
+        def load_set(op, s):
+            load_scales(planes[(op, s)], tensors[op][3], sets[s][0] * H, (sets[s][0] + sets[s][1]) * H)
+
+        def load_act(op):
+            nc.sync.dma_start(out=words[op][:], in_=tensors[op][0].rearrange("g p n -> p g n"))
+
+        def load_w(op, j, h):
+            b0 = 2 * (H * j + HALF * h)
+            nc.sync.dma_start(out=words[(op, j, h)][:],
+                              in_=tensors[op][2][:, :, b0 : b0 + 2 * HALF].rearrange("g p n -> p g n"))
+
+        nc.vector.memset(zero[:], 0.0)
+        zero_planes(nc.vector, planes["m"], 0, GM)
+        zero_planes(nc.vector, planes[("m", 0)], 0, 1)
+        nc.gpsimd.memset(warm[:], 0.0)
+        zero_planes(nc.gpsimd, planes[("m", 0)], 1, GM)
+        zero_planes(nc.gpsimd, planes["x"], 0, GX)
+        zero_planes(nc.vector, planes[("x", 0)], 0, GX)
+        nc.scalar.activation(out=warm[:], in_=warm[:], func=ACT.Sigmoid)
+        nc.gpsimd.dma_start(out=cp[:], in_=c_prev.rearrange("(t p) n -> p t n", p=P))
+        for s in range(1, len(sets)):
+            zero_planes(nc.gpsimd, planes[("m", s)], 0, GM)
+            zero_planes(nc.gpsimd, planes[("x", s)], 0, GX)
+
+        load_act("m")
+        load_w("m", 3, 0)
+        load_scales(planes["m"], m_scales, 0, B)
+        load_set("m", 0)
+        load_w("m", 3, 1)
+        load_w("m", 2, 0)
+        load_act("x")
+        load_w("x", 2, 0)
+        load_scales(planes["x"], x_scales, 0, B)
+        load_set("x", 0)
+        load_w("x", 3, 0)
+        load_set("m", 1)
+        load_set("x", 1)
+        for j in (0, 1):
+            load_w("m", j, 0)
+            load_w("x", j, 0)
+        load_set("m", 2)
+        load_set("x", 2)
+        for j in (4, 5, 6, 7):
+            load_w("m", j, 0)
+            load_w("x", j, 0)
+        for j in (4, 5, 6, 7, 0, 1, 3, 2):
+            if j != 3:
+                load_w("m", j, 1)
+            load_w("x", j, 1)
+
+        junk = psum.tile([P, 512], F32, name="acc")
+        for i in range(WARM):
+            nc.tensor.matmul(out=junk[:], lhsT=zero[:, 0:P], rhs=zero[:], start=True, stop=True)
+
+        def passes(acc, op, t, j, c0, w, first, last):
+            h = c0 // HALF
+            o = c0 - HALF * h
+            s = set_of[j]
+            o_s = (j - sets[s][0]) * H + c0
+            g_n = tensors[op][4]
+            for g in range(g_n):
+                nc.tensor.matmul_mx(
+                    out=acc,
+                    lhsT=words[op][:, g, 2 * P * t : 2 * P * (t + 1)].bitcast(F4X4),
+                    lhsT_scale=planes[op][:, g, P * t : P * (t + 1)],
+                    rhs=words[(op, j, h)][:, g, 2 * o : 2 * (o + w)].bitcast(F4X4),
+                    rhs_scale=planes[(op, s)][:, g, o_s : o_s + w],
+                    start=first and g == 0, stop=last and g == g_n - 1)
+
+        def act(func, a):
+            return lambda o, v: nc.scalar.activation(out=o, in_=v(a), func=func)
+
+        def tt(a, b, op):
+            return lambda o, v: nc.vector.tensor_tensor(out=o, in0=v(a), in1=v(b), op=op)
+
+        def relu_then(a, b, op):
+            return lambda o, v: nc.vector.scalar_tensor_tensor(out=o, in0=v(a), scalar=0.0, in1=v(b), op0=ALU.max, op1=op)
+
+        steps = (
+            ("a4", act(ACT.Tanh, 4), (4,)),
+            ("a5", act(ACT.Sigmoid, 5), (5,)),
+            ("g", tt("a4", "a5", ALU.mult), ("a4", "a5")),
+            ("hh", act(ACT.Tanh, "g"), ("g",)),
+            ("a6", act(ACT.Tanh, 6), (6,)),
+            ("a7", act(ACT.Sigmoid, 7), (7,)),
+            ("i", tt("a6", "a7", ALU.add), ("a6", "a7")),
+            ("jj", act(ACT.Sigmoid, "i"), ("i",)),
+            ("kk", tt("hh", "jj", ALU.add), ("hh", "jj")),
+            ("l", act(ACT.Tanh, "kk"), ("kk",)),
+            ("a0", act(ACT.Sigmoid, 0), (0,)),
+            ("b", relu_then(1, "a0", ALU.mult), (1, "a0")),
+            ("c", act(ACT.Tanh, "b"), ("b",)),
+            ("d", tt("c", "cp", ALU.add), ("c",)),
+            ("e", act(ACT.Tanh, "d"), ("d",)),
+            ("el", tt("e", "l", ALU.mult), ("e", "l")),
+            ("pr", tt(3, "m3", ALU.mult), (3,)),
+            ("a2", act(ACT.Sigmoid, 2), (2,)),
+            ("q", relu_then("pr", "a2", ALU.add), ("pr", "a2")),
+            ("f", act(ACT.Tanh, "q"), ("q",)),
+            ("z", tt("el", "f", ALU.mult), ("el", "f")),
+            ("nc", tt("e", "f", ALU.mult), ("e", "f")),
+            ("nm", act(ACT.Tanh, "z"), ("z",)),
+        )
+        split_steps = ("a2", "q", "f", "z", "nc", "nm")
+
+        units = (
+            dict(t0=0, nt=1, c0=0, w=HALF, split=False, store=nc.gpsimd),
+            dict(t0=1, nt=1, c0=0, w=HALF, split=False, store=nc.gpsimd),
+            dict(t0=0, nt=2, c0=HALF, w=HALF // 2, split=False, store=nc.gpsimd),
+            dict(t0=0, nt=2, c0=HALF + HALF // 2, w=HALF // 2, split=True, store=nc.sync),
+        )
+        groups = [("m3", h, t) for h in range(2) for t in range(2)]
+        groups += [(t, j, t) for j in (2, 3, 0, 1, 4, 5, 6, 7) for t in range(2)]
+        groups += [(u, j, t) for u in (2, 3) for j in (4, 5, 6, 7, 0, 1, 3, 2) for t in range(2)]
+        banks = {}
+        slots = {}
+
+        def at(slot, fn):
+            slots.setdefault(slot, []).append(fn)
+
+        def bank(key):
+            u, j, t = key
+            if u == "m3":
+                name, nt, w = key, 1, HALF
+            else:
+                own = units[u]["nt"] == 1 or (units[u]["split"] and j == 2)
+                name, nt, w = (u, j, t if own else -1), (1 if own else 2), units[u]["w"]
+            if name not in banks:
+                acc = psum.tile([P, nt, w], F32, name="acc")
+                banks[name] = acc
+            return banks[name], (t if nt == 2 else 0)
+
+        def plan(u):
+            t0, nt, c0, w, split, store = [units[u][n] for n in ("t0", "nt", "c0", "w", "split", "store")]
+            tiles = {}
+            slot = {}
+
+            def view(name, a, b):
+                if name == "cp":
+                    return cp[:, t0 + a : t0 + b, c0 : c0 + w]
+                if name == "m3":
+                    return m3[:, t0 + a : t0 + b, c0 : c0 + w]
+                if isinstance(name, int):
+                    acc, i = bank((u, name, t0 + a))
+                    return acc[:, i : i + b - a, :]
+                if name not in tiles:
+                    new = work.tile([P, nt, w], F32, name="v_" + name)
+                    tiles[name] = new
+                return tiles[name][:, a:b, :]
+
+            def emit(name, fn, a, b):
+                def go():
+                    fn(view(name, a, b), lambda n: view(n, a, b))
+                    for key, out in (("nc", new_c), ("nm", new_m)):
+                        if name == key:
+                            dst = out.rearrange("(t p) n -> p t n", p=P)
+                            store.dma_start(out=dst[:, t0 + a : t0 + b, c0 : c0 + w], in_=view(name, a, b))
+                return go
+
+            for name, fn, needs in steps:
+                parts = [(a, a + 1) for a in range(nt)] if split and name in split_steps else [(0, nt)]
+                for a, b in parts:
+                    when = 0
+                    for t in range(a, b):
+                        for need in needs:
+                            if isinstance(need, int):
+                                when = max(when, groups.index((u, need, t0 + t)))
+                            else:
+                                when = max(when, slot[(need, t)] + 1)
+                    for t in range(a, b):
+                        slot[(name, t)] = when
+                    at(when, emit(name, fn, a, b))
+
+        def copy_m3(h, t):
+            return lambda: nc.vector.tensor_copy(out=m3[:, t, HALF * h : HALF * (h + 1)], in_=bank(("m3", h, t))[0][:, 0, :])
+
+        for k in range(4):
+            at(k, copy_m3(groups[k][1], groups[k][2]))
+        for u in range(len(units)):
+            plan(u)
+
+        def run(key, ops):
+            u, j, t = key
+            acc, i = bank(key)
+            if u == "m3":
+                passes(acc[:, i, :], "m", t, 3, HALF * j, HALF, True, True)
+                return
+            c0, w = units[u]["c0"], units[u]["w"]
+            for op in ops:
+                if op == "m" and j != 3:
+                    passes(acc[:, i, :], "m", t, j, c0, w, True, False)
+                if op == "x":
+                    passes(acc[:, i, :], "x", t, j, c0, w, j == 3, True)
+
+        early = groups[4:6]
+        for k in range(len(groups)):
+            if k == 4:
+                for key in early:
+                    run(key, "m")
+            run(groups[k], "x" if groups[k] in early else "mx")
+            for fn in slots.pop(k, []):
+                fn()
+        for k in sorted(slots):
+            for fn in slots[k]:
+                fn()

@@ -14,42 +14,73 @@ B, I, H = 256, 1536, 1024
 FLOPS = 2 * B * 8 * H * (I + H)
 
 P = 128
-GM, GX = H // 512, I // 512
+GROUPS = {"m": H // 512, "x": I // 512}
 HALF = 512
 WARM = 12
+HOP = 3.5
+
+STEPS = (
+    ("a4", "t", "tanh", (4,)),
+    ("a5", "s", "sigmoid", (5,)),
+    ("l1_45", "t", "mult", ("a4", "a5")),
+    ("l2_2", "t", "tanh", ("l1_45",)),
+    ("a6", "u", "tanh", (6,)),
+    ("a7", "s", "sigmoid", (7,)),
+    ("l1_67", "u", "add", ("a6", "a7")),
+    ("l2_3", "u", "sigmoid", ("l1_67",)),
+    ("sum_3", "t", "add", ("l2_2", "l2_3")),
+    ("l3_1", "t", "tanh", ("sum_3",)),
+    ("a0", "c", "sigmoid", (0,)),
+    ("l1_01", "c", "relu_mult", (1, "a0")),
+    ("l2_0a", "c", "tanh", ("l1_01",)),
+    ("sum_c", "c", "add", ("l2_0a", "c_prev")),
+    ("l2_0", "c", "tanh", ("sum_c",)),
+    ("gate", "g", "mult", ("l2_0", "l3_1")),
+    ("prod_3", "p", "mult", (3, "ms_3")),
+    ("a2", "a", "sigmoid", (2,)),
+    ("l1_23", "a", "relu_add", ("prod_3", "a2")),
+    ("l2_1", "a", "tanh", ("l1_23",)),
+    ("z", "z", "mult", ("gate", "l2_1")),
+    ("new_c", "n", "mult", ("l2_0", "l2_1")),
+    ("new_m", "z", "tanh", ("z",)),
+)
+LATE = (0, 1, 3, 2)
 
 
 def tile_nascell_kernel(tc, x_words, x_scales, m_words, m_scales, c_prev,
                                     wm_words, wm_scales, wx_words, wx_scales, new_m, new_c):
     nc = tc.nc
+    act_words = {"m": m_words, "x": x_words}
+    act_scales = {"m": m_scales, "x": x_scales}
+    w_words = {"m": wm_words, "x": wx_words}
+    w_scales = {"m": wm_scales, "x": wx_scales}
+    outs = {"new_m": new_m, "new_c": new_c}
+
     with ExitStack() as ctx:
         keep = ctx.enter_context(tc.tile_pool(name="keep", bufs=1))
-        work = ctx.enter_context(tc.tile_pool(name="work", bufs=2))
+        work = ctx.enter_context(tc.tile_pool(name="work", bufs=4))
         psum = ctx.enter_context(tc.psum_pool(name="psum", bufs=8))
         ctx.enter_context(tc.manual_schedule())
 
         words, planes = {}, {}
-        tensors = {"m": (m_words, m_scales, wm_words, wm_scales, GM),
-                   "x": (x_words, x_scales, wx_words, wx_scales, GX)}
-        sets = ((2, 2), (0, 2), (4, 4))
+        sets = {"m": ((3, 2), (5, 3), (0, 3)), "x": ((4, 2), (6, 2), (0, 4))}
         set_of = {}
-        for s in range(len(sets)):
-            for j in range(sets[s][0], sets[s][0] + sets[s][1]):
-                set_of[j] = s
         for op in ("m", "x"):
-            g_n = tensors[op][4]
-            t_w = keep.tile([P, g_n, 2 * B], U8, name="aw_" + op, align_bytes=64)
+            n_g = GROUPS[op]
+            t_w = keep.tile([P, n_g, 2 * B], U8, name="aw_" + op, align_bytes=64)
             words[op] = t_w
-            t_p = keep.tile([P, g_n, B], U8, name="ap_" + op, align_bytes=64)
+            t_p = keep.tile([P, n_g, B], U8, name="ap_" + op, align_bytes=64)
             planes[op] = t_p
-            for s in range(len(sets)):
-                t_s = keep.tile([P, g_n, sets[s][1] * H], U8, name="wp_%s%d" % (op, s), align_bytes=64)
+            for s in range(len(sets[op])):
+                t_s = keep.tile([P, n_g, sets[op][s][1] * H], U8, name="wp_%s%d" % (op, s), align_bytes=64)
                 planes[(op, s)] = t_s
+                for j in range(sets[op][s][0], sets[op][s][0] + sets[op][s][1]):
+                    set_of[(op, j)] = s
             for j in range(8):
                 for h in range(2):
-                    t_ww = keep.tile([P, g_n, 2 * HALF], U8, name="ww_%s%d%d" % (op, j, h), align_bytes=64)
+                    t_ww = keep.tile([P, n_g, 2 * HALF], U8, name="ww_%s%d%d" % (op, j, h), align_bytes=64)
                     words[(op, j, h)] = t_ww
-        m3 = keep.tile([P, 2, H], F32, name="m3")
+        ms_3 = keep.tile([P, 2, H], F32, name="ms_3")
         cp = keep.tile([P, 2, H], BF16, name="cp")
         zero = keep.tile([P, 512], BF16, name="zero")
         warm = keep.tile([P, 8], F32, name="warm")
@@ -57,214 +88,175 @@ def tile_nascell_kernel(tc, x_words, x_scales, m_words, m_scales, c_prev,
         def zero_planes(engine, tile, g0, g1):
             engine.memset(tile[:, g0:g1, :].rearrange("p g n -> p (g n)").bitcast(I32), 0)
 
-        def load_scales(dst, src, c0, c1):
-            for q in range(4):
+        def load_scales(dst, src, c0, c1, rows):
+            for r in rows:
                 nc.sync.dma_start(
-                    out=dst[32 * q : 32 * q + 4, :, :].bitcast(I32),
-                    in_=src[:, 4 * q : 4 * q + 4, c0:c1].rearrange("g r n -> r g n").bitcast(I32))
+                    out=dst[r:P:32, :, :].bitcast(I32),
+                    in_=src[:, r:16:4, c0:c1].rearrange("g q n -> q g n").bitcast(I32))
 
-        def load_set(op, s):
-            load_scales(planes[(op, s)], tensors[op][3], sets[s][0] * H, (sets[s][0] + sets[s][1]) * H)
+        def load_set(op, s, rows):
+            first, count = sets[op][s]
+            load_scales(planes[(op, s)], w_scales[op], first * H, (first + count) * H, rows)
 
         def load_act(op):
-            nc.sync.dma_start(out=words[op][:], in_=tensors[op][0].rearrange("g p n -> p g n"))
+            nc.sync.dma_start(out=words[op][:], in_=act_words[op].rearrange("g p n -> p g n"))
 
         def load_w(op, j, h):
             b0 = 2 * (H * j + HALF * h)
             nc.sync.dma_start(out=words[(op, j, h)][:],
-                              in_=tensors[op][2][:, :, b0 : b0 + 2 * HALF].rearrange("g p n -> p g n"))
+                              in_=w_words[op][:, :, b0 : b0 + 2 * HALF].rearrange("g p n -> p g n"))
 
+        every = range(4)
         nc.vector.memset(zero[:], 0.0)
-        zero_planes(nc.vector, planes["m"], 0, GM)
+        zero_planes(nc.vector, planes["m"], 0, 2)
         zero_planes(nc.vector, planes[("m", 0)], 0, 1)
         nc.gpsimd.memset(warm[:], 0.0)
-        zero_planes(nc.gpsimd, planes[("m", 0)], 1, GM)
-        zero_planes(nc.gpsimd, planes["x"], 0, GX)
-        zero_planes(nc.vector, planes[("x", 0)], 0, GX)
+        zero_planes(nc.gpsimd, planes[("m", 0)], 1, 2)
+        zero_planes(nc.gpsimd, planes["x"], 0, 3)
+        zero_planes(nc.vector, planes[("x", 0)], 0, 3)
         nc.scalar.activation(out=warm[:], in_=warm[:], func=ACT.Sigmoid)
         nc.gpsimd.dma_start(out=cp[:], in_=c_prev.rearrange("(t p) n -> p t n", p=P))
-        for s in range(1, len(sets)):
-            zero_planes(nc.gpsimd, planes[("m", s)], 0, GM)
-            zero_planes(nc.gpsimd, planes[("x", s)], 0, GX)
+        for s in range(1, 3):
+            zero_planes(nc.gpsimd, planes[("m", s)], 0, 2)
+            zero_planes(nc.gpsimd, planes[("x", s)], 0, 3)
 
         load_act("m")
         load_w("m", 3, 0)
-        load_scales(planes["m"], m_scales, 0, B)
-        load_set("m", 0)
+        load_scales(planes["m"], m_scales, 0, B, every)
+        load_set("m", 0, every)
         load_w("m", 3, 1)
-        load_w("m", 2, 0)
+        load_w("m", 4, 0)
         load_act("x")
-        load_w("x", 2, 0)
-        load_scales(planes["x"], x_scales, 0, B)
-        load_set("x", 0)
-        load_w("x", 3, 0)
-        load_set("m", 1)
-        load_set("x", 1)
-        for j in (0, 1):
-            load_w("m", j, 0)
-            load_w("x", j, 0)
-        load_set("m", 2)
-        load_set("x", 2)
-        for j in (4, 5, 6, 7):
-            load_w("m", j, 0)
-            load_w("x", j, 0)
-        for j in (4, 5, 6, 7, 0, 1, 3, 2):
-            if j != 3:
-                load_w("m", j, 1)
-            load_w("x", j, 1)
+        load_w("x", 4, 0)
+        load_scales(planes["x"], x_scales, 0, B, every)
+        load_set("x", 0, every)
+        load_w("m", 4, 1)
+        load_w("x", 4, 1)
+        stream = [(op, j, h) for j in (5, 6, 7) for h in range(2) for op in ("m", "x")]
+        stream += [(op, j, h) for h in range(2) for j in LATE for op in ("m", "x") if (op, j) != ("m", 3)]
+        rest = [(op, s, r) for s in (1, 2) for r in range(4) for op in ("m", "x")]
+        for i in range(len(stream)):
+            if i < len(rest):
+                load_set(rest[i][0], rest[i][1], (rest[i][2],))
+            load_w(stream[i][0], stream[i][1], stream[i][2])
 
         junk = psum.tile([P, 512], F32, name="acc")
         for i in range(WARM):
             nc.tensor.matmul(out=junk[:], lhsT=zero[:, 0:P], rhs=zero[:], start=True, stop=True)
 
-        def passes(acc, op, t, j, c0, w, first, last):
-            h = c0 // HALF
-            o = c0 - HALF * h
-            s = set_of[j]
-            o_s = (j - sets[s][0]) * H + c0
-            g_n = tensors[op][4]
-            for g in range(g_n):
+        def cuts(u, j):
+            return ((0, 256), (256, 512)) if u == 3 and j in LATE else ((0, HALF),)
+
+        order = [("m3", u, 0, HALF, "m") for u in range(4)]
+        order += [(4, u, 0, HALF, "m") for u in range(4)]
+        order += [(j, u, 0, HALF, "x" if j == 4 else "mx") for j in (4, 5, 6, 7) for u in range(4)]
+        for u in range(4):
+            if u < 3:
+                order += [(j, u, 0, HALF, "mx") for j in LATE]
+            else:
+                order += [(j, u, a, b, "mx") for a, b in ((0, 256), (256, 512)) for j in LATE]
+
+        banks = {}
+
+        def bank(j, u, a, b):
+            if (j, u, a) not in banks:
+                acc = psum.tile([P, b - a], F32, name="acc")
+                banks[(j, u, a)] = acc
+            return banks[(j, u, a)]
+
+        def run(j, u, a, b, ops):
+            t, h = u % 2, u // 2
+            piece = 3 if j == "m3" else j
+            if j == 3:
+                ops = "x"
+            jobs = [(op, g) for op in ops for g in range(GROUPS[op])]
+            acc = bank(j, u, a, b)
+            for i in range(len(jobs)):
+                op, g = jobs[i]
+                s = set_of[(op, piece)]
+                o = (piece - sets[op][s][0]) * H + HALF * h
                 nc.tensor.matmul_mx(
-                    out=acc,
+                    out=acc[:],
                     lhsT=words[op][:, g, 2 * P * t : 2 * P * (t + 1)].bitcast(F4X4),
                     lhsT_scale=planes[op][:, g, P * t : P * (t + 1)],
-                    rhs=words[(op, j, h)][:, g, 2 * o : 2 * (o + w)].bitcast(F4X4),
-                    rhs_scale=planes[(op, s)][:, g, o_s : o_s + w],
-                    start=first and g == 0, stop=last and g == g_n - 1)
+                    rhs=words[(op, piece, h)][:, g, 2 * a : 2 * b].bitcast(F4X4),
+                    rhs_scale=planes[(op, s)][:, g, o + a : o + b],
+                    start=i == 0 and not (j == 4 and ops == "x"),
+                    stop=i == len(jobs) - 1 and not (j == 4 and ops == "m"))
 
-        def act(func, a):
-            return lambda o, v: nc.scalar.activation(out=o, in_=v(a), func=func)
+        ends = {}
+        total = 0.0
+        for j, u, a, b, ops in order:
+            passes = sum([GROUPS[op] for op in ("x" if j == 3 else ops)])
+            total += passes * (b - a) / 512.0
+            ends[(j, u, a)] = total
 
-        def tt(a, b, op):
-            return lambda o, v: nc.vector.tensor_tensor(out=o, in0=v(a), in1=v(b), op=op)
+        tiles = {}
+        home = {}
+        for name, tag, kind, needs in STEPS:
+            home[name] = tag
 
-        def relu_then(a, b, op):
-            return lambda o, v: nc.vector.scalar_tensor_tensor(out=o, in0=v(a), scalar=0.0, in1=v(b), op0=ALU.max, op1=op)
+        def view(name, u, a, b):
+            t, h = u % 2, u // 2
+            if name == "ms_3":
+                return ms_3[:, t, HALF * h + a : HALF * h + b]
+            if name == "c_prev":
+                return cp[:, t, HALF * h + a : HALF * h + b]
+            if name in home:
+                key = (name if home[name] == "s" else home[name], u)
+                if key not in tiles:
+                    new = work.tile([P, HALF], F32, name="v_" + home[name])
+                    tiles[key] = new
+                return tiles[key][:, a:b]
+            return bank(name, u, a, b)[:]
 
-        steps = (
-            ("a4", act(ACT.Tanh, 4), (4,)),
-            ("a5", act(ACT.Sigmoid, 5), (5,)),
-            ("g", tt("a4", "a5", ALU.mult), ("a4", "a5")),
-            ("hh", act(ACT.Tanh, "g"), ("g",)),
-            ("a6", act(ACT.Tanh, 6), (6,)),
-            ("a7", act(ACT.Sigmoid, 7), (7,)),
-            ("i", tt("a6", "a7", ALU.add), ("a6", "a7")),
-            ("jj", act(ACT.Sigmoid, "i"), ("i",)),
-            ("kk", tt("hh", "jj", ALU.add), ("hh", "jj")),
-            ("l", act(ACT.Tanh, "kk"), ("kk",)),
-            ("a0", act(ACT.Sigmoid, 0), (0,)),
-            ("b", relu_then(1, "a0", ALU.mult), (1, "a0")),
-            ("c", act(ACT.Tanh, "b"), ("b",)),
-            ("d", tt("c", "cp", ALU.add), ("c",)),
-            ("e", act(ACT.Tanh, "d"), ("d",)),
-            ("el", tt("e", "l", ALU.mult), ("e", "l")),
-            ("pr", tt(3, "m3", ALU.mult), (3,)),
-            ("a2", act(ACT.Sigmoid, 2), (2,)),
-            ("q", relu_then("pr", "a2", ALU.add), ("pr", "a2")),
-            ("f", act(ACT.Tanh, "q"), ("q",)),
-            ("z", tt("el", "f", ALU.mult), ("el", "f")),
-            ("nc", tt("e", "f", ALU.mult), ("e", "f")),
-            ("nm", act(ACT.Tanh, "z"), ("z",)),
-        )
-        split_steps = ("a2", "q", "f", "z", "nc", "nm")
+        todo = []
+        for u in range(4):
+            todo.append((ends[("m3", u, 0)], len(todo), "ms_3", "copy", ("m3",), u, 0, HALF))
+        for u in range(4):
+            when = {}
+            for name, tag, kind, needs in STEPS:
+                late = name in ("a0", "l1_01", "l2_0a", "sum_c", "l2_0", "gate", "prod_3", "a2", "l1_23", "l2_1", "z", "new_c", "new_m")
+                for a, b in (((0, 256), (256, 512)) if u == 3 and late else ((0, HALF),)):
+                    start = 0.0
+                    for need in needs:
+                        if (need, u, a) in ends:
+                            start = max(start, ends[(need, u, a)])
+                        elif (need, a) in when:
+                            start = max(start, when[(need, a)] + HOP * (0.4 + 0.6 * (b - a) / 512.0))
+                        elif (need, 0) in when:
+                            start = max(start, when[(need, 0)] + HOP)
+                    when[(name, a)] = start
+                    todo.append((start, len(todo), name, kind, needs, u, a, b))
+        todo.sort()
 
-        units = (
-            dict(t0=0, nt=1, c0=0, w=HALF, split=False, store=nc.gpsimd),
-            dict(t0=1, nt=1, c0=0, w=HALF, split=False, store=nc.gpsimd),
-            dict(t0=0, nt=2, c0=HALF, w=HALF // 2, split=False, store=nc.gpsimd),
-            dict(t0=0, nt=2, c0=HALF + HALF // 2, w=HALF // 2, split=True, store=nc.sync),
-        )
-        groups = [("m3", h, t) for h in range(2) for t in range(2)]
-        groups += [(t, j, t) for j in (2, 3, 0, 1, 4, 5, 6, 7) for t in range(2)]
-        groups += [(u, j, t) for u in (2, 3) for j in (4, 5, 6, 7, 0, 1, 3, 2) for t in range(2)]
-        banks = {}
-        slots = {}
-
-        def at(slot, fn):
-            slots.setdefault(slot, []).append(fn)
-
-        def bank(key):
-            u, j, t = key
-            if u == "m3":
-                name, nt, w = key, 1, HALF
+        def step(name, kind, needs, u, a, b):
+            out = view(name, u, a, b)
+            src = [view(need, u, a, b) for need in needs]
+            if kind == "tanh":
+                nc.scalar.activation(out=out, in_=src[0], func=ACT.Tanh)
+            elif kind == "sigmoid":
+                nc.scalar.activation(out=out, in_=src[0], func=ACT.Sigmoid)
+            elif kind == "mult":
+                nc.vector.tensor_tensor(out=out, in0=src[0], in1=src[1], op=ALU.mult)
+            elif kind == "add":
+                nc.vector.tensor_tensor(out=out, in0=src[0], in1=src[1], op=ALU.add)
+            elif kind == "relu_mult":
+                nc.vector.scalar_tensor_tensor(out=out, in0=src[0], scalar=0.0, in1=src[1], op0=ALU.max, op1=ALU.mult)
+            elif kind == "relu_add":
+                nc.vector.scalar_tensor_tensor(out=out, in0=src[0], scalar=0.0, in1=src[1], op0=ALU.max, op1=ALU.add)
             else:
-                own = units[u]["nt"] == 1 or (units[u]["split"] and j == 2)
-                name, nt, w = (u, j, t if own else -1), (1 if own else 2), units[u]["w"]
-            if name not in banks:
-                acc = psum.tile([P, nt, w], F32, name="acc")
-                banks[name] = acc
-            return banks[name], (t if nt == 2 else 0)
+                nc.vector.tensor_copy(out=out, in_=src[0])
+            if name in outs:
+                t, h = u % 2, u // 2
+                nc.sync.dma_start(out=outs[name][P * t : P * (t + 1), HALF * h + a : HALF * h + b], in_=out)
 
-        def plan(u):
-            t0, nt, c0, w, split, store = [units[u][n] for n in ("t0", "nt", "c0", "w", "split", "store")]
-            tiles = {}
-            slot = {}
-
-            def view(name, a, b):
-                if name == "cp":
-                    return cp[:, t0 + a : t0 + b, c0 : c0 + w]
-                if name == "m3":
-                    return m3[:, t0 + a : t0 + b, c0 : c0 + w]
-                if isinstance(name, int):
-                    acc, i = bank((u, name, t0 + a))
-                    return acc[:, i : i + b - a, :]
-                if name not in tiles:
-                    new = work.tile([P, nt, w], F32, name="v_" + name)
-                    tiles[name] = new
-                return tiles[name][:, a:b, :]
-
-            def emit(name, fn, a, b):
-                def go():
-                    fn(view(name, a, b), lambda n: view(n, a, b))
-                    for key, out in (("nc", new_c), ("nm", new_m)):
-                        if name == key:
-                            dst = out.rearrange("(t p) n -> p t n", p=P)
-                            store.dma_start(out=dst[:, t0 + a : t0 + b, c0 : c0 + w], in_=view(name, a, b))
-                return go
-
-            for name, fn, needs in steps:
-                parts = [(a, a + 1) for a in range(nt)] if split and name in split_steps else [(0, nt)]
-                for a, b in parts:
-                    when = 0
-                    for t in range(a, b):
-                        for need in needs:
-                            if isinstance(need, int):
-                                when = max(when, groups.index((u, need, t0 + t)))
-                            else:
-                                when = max(when, slot[(need, t)] + 1)
-                    for t in range(a, b):
-                        slot[(name, t)] = when
-                    at(when, emit(name, fn, a, b))
-
-        def copy_m3(h, t):
-            return lambda: nc.vector.tensor_copy(out=m3[:, t, HALF * h : HALF * (h + 1)], in_=bank(("m3", h, t))[0][:, 0, :])
-
-        for k in range(4):
-            at(k, copy_m3(groups[k][1], groups[k][2]))
-        for u in range(len(units)):
-            plan(u)
-
-        def run(key, ops):
-            u, j, t = key
-            acc, i = bank(key)
-            if u == "m3":
-                passes(acc[:, i, :], "m", t, 3, HALF * j, HALF, True, True)
-                return
-            c0, w = units[u]["c0"], units[u]["w"]
-            for op in ops:
-                if op == "m" and j != 3:
-                    passes(acc[:, i, :], "m", t, j, c0, w, True, False)
-                if op == "x":
-                    passes(acc[:, i, :], "x", t, j, c0, w, j == 3, True)
-
-        early = groups[4:6]
-        for k in range(len(groups)):
-            if k == 4:
-                for key in early:
-                    run(key, "m")
-            run(groups[k], "x" if groups[k] in early else "mx")
-            for fn in slots.pop(k, []):
-                fn()
-        for k in sorted(slots):
-            for fn in slots[k]:
-                fn()
+        at = 0
+        for j, u, a, b, ops in order:
+            run(j, u, a, b, ops)
+            while not (j == 4 and ops == "m") and at < len(todo) and todo[at][0] <= ends[(j, u, a)]:
+                step(*todo[at][2:])
+                at += 1
+        while at < len(todo):
+            step(*todo[at][2:])
+            at += 1

from contextlib import ExitStack

import concourse.mybir as mybir

F32 = mybir.dt.float32
BF16 = mybir.dt.bfloat16
I32 = mybir.dt.int32
U8 = mybir.dt.uint8
F4X4 = mybir.dt.float4_e2m1fn_x4
ACT = mybir.ActivationFunctionType
ALU = mybir.AluOpType

B, I, H = 256, 1536, 1024
FLOPS = 2 * B * 8 * H * (I + H)

P = 128
GROUPS = {"m": H // 512, "x": I // 512}
HALF = 512
WARM = 12
HOP = 3.5

STEPS = (
    ("a4", "t", "tanh", (4,)),
    ("a5", "s", "sigmoid", (5,)),
    ("l1_45", "t", "mult", ("a4", "a5")),
    ("l2_2", "t", "tanh", ("l1_45",)),
    ("a6", "u", "tanh", (6,)),
    ("a7", "s", "sigmoid", (7,)),
    ("l1_67", "u", "add", ("a6", "a7")),
    ("l2_3", "u", "sigmoid", ("l1_67",)),
    ("sum_3", "t", "add", ("l2_2", "l2_3")),
    ("l3_1", "t", "tanh", ("sum_3",)),
    ("a0", "c", "sigmoid", (0,)),
    ("l1_01", "c", "relu_mult", (1, "a0")),
    ("l2_0a", "c", "tanh", ("l1_01",)),
    ("sum_c", "c", "add", ("l2_0a", "c_prev")),
    ("l2_0", "c", "tanh", ("sum_c",)),
    ("gate", "g", "mult", ("l2_0", "l3_1")),
    ("prod_3", "p", "mult", (3, "ms_3")),
    ("a2", "a", "sigmoid", (2,)),
    ("l1_23", "a", "relu_add", ("prod_3", "a2")),
    ("l2_1", "a", "tanh", ("l1_23",)),
    ("z", "z", "mult", ("gate", "l2_1")),
    ("new_c", "n", "mult", ("l2_0", "l2_1")),
    ("new_m", "z", "tanh", ("z",)),
)
LATE = (0, 1, 3, 2)


def tile_nascell_kernel(tc, x_words, x_scales, m_words, m_scales, c_prev,
                                    wm_words, wm_scales, wx_words, wx_scales, new_m, new_c):
    nc = tc.nc
    act_words = {"m": m_words, "x": x_words}
    act_scales = {"m": m_scales, "x": x_scales}
    w_words = {"m": wm_words, "x": wx_words}
    w_scales = {"m": wm_scales, "x": wx_scales}
    outs = {"new_m": new_m, "new_c": new_c}

    with ExitStack() as ctx:
        keep = ctx.enter_context(tc.tile_pool(name="keep", bufs=1))
        work = ctx.enter_context(tc.tile_pool(name="work", bufs=4))
        psum = ctx.enter_context(tc.psum_pool(name="psum", bufs=8))
        ctx.enter_context(tc.manual_schedule())

        words, planes = {}, {}
        sets = {"m": ((3, 2), (5, 3), (0, 3)), "x": ((4, 2), (6, 2), (0, 4))}
        set_of = {}
        for op in ("m", "x"):
            n_g = GROUPS[op]
            t_w = keep.tile([P, n_g, 2 * B], U8, name="aw_" + op, align_bytes=64)
            words[op] = t_w
            t_p = keep.tile([P, n_g, B], U8, name="ap_" + op, align_bytes=64)
            planes[op] = t_p
            for s in range(len(sets[op])):
                t_s = keep.tile([P, n_g, sets[op][s][1] * H], U8, name="wp_%s%d" % (op, s), align_bytes=64)
                planes[(op, s)] = t_s
                for j in range(sets[op][s][0], sets[op][s][0] + sets[op][s][1]):
                    set_of[(op, j)] = s
            for j in range(8):
                for h in range(2):
                    t_ww = keep.tile([P, n_g, 2 * HALF], U8, name="ww_%s%d%d" % (op, j, h), align_bytes=64)
                    words[(op, j, h)] = t_ww
        ms_3 = keep.tile([P, 2, H], F32, name="ms_3")
        cp = keep.tile([P, 2, H], BF16, name="cp")
        zero = keep.tile([P, 512], BF16, name="zero")
        warm = keep.tile([P, 8], F32, name="warm")

        def zero_planes(engine, tile, g0, g1):
            engine.memset(tile[:, g0:g1, :].rearrange("p g n -> p (g n)").bitcast(I32), 0)

        def load_scales(dst, src, c0, c1, rows):
            for r in rows:
                nc.sync.dma_start(
                    out=dst[r:P:32, :, :].bitcast(I32),
                    in_=src[:, r:16:4, c0:c1].rearrange("g q n -> q g n").bitcast(I32))

        def load_set(op, s, rows):
            first, count = sets[op][s]
            load_scales(planes[(op, s)], w_scales[op], first * H, (first + count) * H, rows)

        def load_act(op):
            nc.sync.dma_start(out=words[op][:], in_=act_words[op].rearrange("g p n -> p g n"))

        def load_w(op, j, h):
            b0 = 2 * (H * j + HALF * h)
            nc.sync.dma_start(out=words[(op, j, h)][:],
                              in_=w_words[op][:, :, b0 : b0 + 2 * HALF].rearrange("g p n -> p g n"))

        every = range(4)
        nc.vector.memset(zero[:], 0.0)
        zero_planes(nc.vector, planes["m"], 0, 2)
        zero_planes(nc.vector, planes[("m", 0)], 0, 1)
        nc.gpsimd.memset(warm[:], 0.0)
        zero_planes(nc.gpsimd, planes[("m", 0)], 1, 2)
        zero_planes(nc.gpsimd, planes["x"], 0, 3)
        zero_planes(nc.vector, planes[("x", 0)], 0, 3)
        nc.scalar.activation(out=warm[:], in_=warm[:], func=ACT.Sigmoid)
        nc.gpsimd.dma_start(out=cp[:], in_=c_prev.rearrange("(t p) n -> p t n", p=P))
        for s in range(1, 3):
            zero_planes(nc.gpsimd, planes[("m", s)], 0, 2)
            zero_planes(nc.gpsimd, planes[("x", s)], 0, 3)

        load_act("m")
        load_w("m", 3, 0)
        load_scales(planes["m"], m_scales, 0, B, every)
        load_set("m", 0, every)
        load_w("m", 3, 1)
        load_w("m", 4, 0)
        load_act("x")
        load_w("x", 4, 0)
        load_scales(planes["x"], x_scales, 0, B, every)
        load_set("x", 0, every)
        load_w("m", 4, 1)
        load_w("x", 4, 1)
        stream = [(op, j, h) for j in (5, 6, 7) for h in range(2) for op in ("m", "x")]
        stream += [(op, j, h) for h in range(2) for j in LATE for op in ("m", "x") if (op, j) != ("m", 3)]
        rest = [(op, s, r) for s in (1, 2) for r in range(4) for op in ("m", "x")]
        for i in range(len(stream)):
            if i < len(rest):
                load_set(rest[i][0], rest[i][1], (rest[i][2],))
            load_w(stream[i][0], stream[i][1], stream[i][2])

        junk = psum.tile([P, 512], F32, name="acc")
        for i in range(WARM):
            nc.tensor.matmul(out=junk[:], lhsT=zero[:, 0:P], rhs=zero[:], start=True, stop=True)

        def cuts(u, j):
            return ((0, 256), (256, 512)) if u == 3 and j in LATE else ((0, HALF),)

        order = [("m3", u, 0, HALF, "m") for u in range(4)]
        order += [(4, u, 0, HALF, "m") for u in range(4)]
        order += [(j, u, 0, HALF, "x" if j == 4 else "mx") for j in (4, 5, 6, 7) for u in range(4)]
        for u in range(4):
            if u < 3:
                order += [(j, u, 0, HALF, "mx") for j in LATE]
            else:
                order += [(j, u, a, b, "mx") for a, b in ((0, 256), (256, 512)) for j in LATE]

        banks = {}

        def bank(j, u, a, b):
            if (j, u, a) not in banks:
                acc = psum.tile([P, b - a], F32, name="acc")
                banks[(j, u, a)] = acc
            return banks[(j, u, a)]

        def run(j, u, a, b, ops):
            t, h = u % 2, u // 2
            piece = 3 if j == "m3" else j
            if j == 3:
                ops = "x"
            jobs = [(op, g) for op in ops for g in range(GROUPS[op])]
            acc = bank(j, u, a, b)
            for i in range(len(jobs)):
                op, g = jobs[i]
                s = set_of[(op, piece)]
                o = (piece - sets[op][s][0]) * H + HALF * h
                nc.tensor.matmul_mx(
                    out=acc[:],
                    lhsT=words[op][:, g, 2 * P * t : 2 * P * (t + 1)].bitcast(F4X4),
                    lhsT_scale=planes[op][:, g, P * t : P * (t + 1)],
                    rhs=words[(op, piece, h)][:, g, 2 * a : 2 * b].bitcast(F4X4),
                    rhs_scale=planes[(op, s)][:, g, o + a : o + b],
                    start=i == 0 and not (j == 4 and ops == "x"),
                    stop=i == len(jobs) - 1 and not (j == 4 and ops == "m"))

        ends = {}
        total = 0.0
        for j, u, a, b, ops in order:
            passes = sum([GROUPS[op] for op in ("x" if j == 3 else ops)])
            total += passes * (b - a) / 512.0
            ends[(j, u, a)] = total

        tiles = {}
        home = {}
        for name, tag, kind, needs in STEPS:
            home[name] = tag

        def view(name, u, a, b):
            t, h = u % 2, u // 2
            if name == "ms_3":
                return ms_3[:, t, HALF * h + a : HALF * h + b]
            if name == "c_prev":
                return cp[:, t, HALF * h + a : HALF * h + b]
            if name in home:
                key = (name if home[name] == "s" else home[name], u)
                if key not in tiles:
                    new = work.tile([P, HALF], F32, name="v_" + home[name])
                    tiles[key] = new
                return tiles[key][:, a:b]
            return bank(name, u, a, b)[:]

        todo = []
        for u in range(4):
            todo.append((ends[("m3", u, 0)], len(todo), "ms_3", "copy", ("m3",), u, 0, HALF))
        for u in range(4):
            when = {}
            for name, tag, kind, needs in STEPS:
                late = name in ("a0", "l1_01", "l2_0a", "sum_c", "l2_0", "gate", "prod_3", "a2", "l1_23", "l2_1", "z", "new_c", "new_m")
                for a, b in (((0, 256), (256, 512)) if u == 3 and late else ((0, HALF),)):
                    start = 0.0
                    for need in needs:
                        if (need, u, a) in ends:
                            start = max(start, ends[(need, u, a)])
                        elif (need, a) in when:
                            start = max(start, when[(need, a)] + HOP * (0.4 + 0.6 * (b - a) / 512.0))
                        elif (need, 0) in when:
                            start = max(start, when[(need, 0)] + HOP)
                    when[(name, a)] = start
                    todo.append((start, len(todo), name, kind, needs, u, a, b))
        todo.sort()

        def step(name, kind, needs, u, a, b):
            out = view(name, u, a, b)
            src = [view(need, u, a, b) for need in needs]
            if kind == "tanh":
                nc.scalar.activation(out=out, in_=src[0], func=ACT.Tanh)
            elif kind == "sigmoid":
                nc.scalar.activation(out=out, in_=src[0], func=ACT.Sigmoid)
            elif kind == "mult":
                nc.vector.tensor_tensor(out=out, in0=src[0], in1=src[1], op=ALU.mult)
            elif kind == "add":
                nc.vector.tensor_tensor(out=out, in0=src[0], in1=src[1], op=ALU.add)
            elif kind == "relu_mult":
                nc.vector.scalar_tensor_tensor(out=out, in0=src[0], scalar=0.0, in1=src[1], op0=ALU.max, op1=ALU.mult)
            elif kind == "relu_add":
                nc.vector.scalar_tensor_tensor(out=out, in0=src[0], scalar=0.0, in1=src[1], op0=ALU.max, op1=ALU.add)
            else:
                nc.vector.tensor_copy(out=out, in_=src[0])
            if name in outs:
                t, h = u % 2, u // 2
                nc.sync.dma_start(out=outs[name][P * t : P * (t + 1), HALF * h + a : HALF * h + b], in_=out)

        at = 0
        for j, u, a, b, ops in order:
            run(j, u, a, b, ops)
            while not (j == 4 and ops == "m") and at < len(todo) and todo[at][0] <= ends[(j, u, a)]:
                step(*todo[at][2:])
                at += 1
        while at < len(todo):
            step(*todo[at][2:])
            at += 1
